import numpy as np
import ml_dtypes


def mxq(x, axis, fmt="e4m3"):
    dtype, down = {"e4m3": (ml_dtypes.float8_e4m3fn, 7), "e5m2": (ml_dtypes.float8_e5m2, 14)}[fmt]
    v = np.moveaxis(np.asarray(x, np.float32).astype(ml_dtypes.bfloat16).astype(np.float64), axis, -1)
    blocks = v.reshape(v.shape[:-1] + (-1, 32))
    amax = np.abs(blocks).max(-1, keepdims=True)
    byte = np.maximum(np.where(amax > 0, np.frexp(amax)[1] - 1 + 127, 0) - down, 1)
    scale = np.exp2(byte - 127.0)
    codes = (blocks / scale).astype(np.float32).astype(dtype).astype(np.float64)
    return np.moveaxis((codes * scale).reshape(v.shape), -1, axis)


WIDE = False


def mx_kscale(k):
    if not WIDE:
        return np.ones(k)
    levels = np.array([10, -10, 5, -5, 0])
    if k % 512:
        return np.exp2(np.random.permutation(np.resize(levels, k // 32))).repeat(32)
    a = np.empty((k // 512, 16))
    for p in range(k // 512):
        a[p, :8] = np.random.permutation(np.resize(levels, 8))
        for g in range(8):
            far = levels[np.abs(levels - a[p, g]) >= 10]
            a[p, g + 8] = far[np.random.randint(len(far))]
    return np.exp2(a.ravel()).repeat(32)


BF16 = ml_dtypes.bfloat16


def bf(x):
    return np.asarray(x, np.float32).astype(BF16)


def f64(x):
    return np.asarray(x).astype(np.float64)


B, S, D, E = 2, 512, 512, 128


def setup_inputs():
    s, t = mx_kscale(S), mx_kscale(D)
    return {"q": bf(np.random.standard_normal((B, S, D)) / t),
            "k": bf(np.random.standard_normal((B, S, D)) * s[:, None] * t),
            "v": bf(np.random.standard_normal((B, S, E)) / s[:, None])}


def reference(q, k, v):
    scale = 1.0 / np.sqrt(q.shape[1])
    qn = f64(q) * scale
    kn = f64(k) * scale
    kv_mat = mxq(kn, 1, "e4m3").transpose(0, 2, 1) @ mxq(f64(v), 1, "e4m3")
    out = mxq(qn, 2, "e4m3") @ mxq(kv_mat, 1, "e4m3")
    return out

@@ -1,0 +1,177 @@
+import math
+from contextlib import ExitStack
+
+import concourse.mybir as mybir
+from concourse.masks import make_identity
+
+BF16 = mybir.dt.bfloat16
+F32 = mybir.dt.float32
+U32 = mybir.dt.uint32
+U8 = mybir.dt.uint8
+FP8X4 = mybir.dt.float8_e4m3fn_x4
+
+B, S, D, E = 2, 512, 512, 128
+P = 128
+PACK = 4
+PAIRS = D // 2
+HALVES = 2
+ROWS = 2
+
+FLOPS = 2 * 2 * B * S * D * E
+SCALE = 1.0 / math.sqrt(S)
+
+K_GROUPS_ON_VECTOR = 84
+
+
+def tile_efficientattention_s_kernel(tc, q, k, v, out):
+    nc = tc.nc
+    with ExitStack() as ctx:
+        keep = ctx.enter_context(tc.tile_pool(name="keep", bufs=1))
+        qt_banks = ctx.enter_context(tc.psum_pool(name="qt_banks", bufs=B * HALVES))
+        kv_banks = ctx.enter_context(tc.psum_pool(name="kv_banks", bufs=B))
+        out_banks = ctx.enter_context(tc.psum_pool(name="out_banks", bufs=2))
+        ctx.enter_context(tc.manual_schedule())
+
+        v_raw = keep.tile([P, B, PACK, E], BF16)
+        nc.sync.dma_start(out=v_raw[:], in_=v.rearrange("b (p j) e -> p b j e", j=PACK))
+        k_raw = {}
+        q_raw = {}
+        for b in range(B):
+            k_raw[b] = keep.tile([P, PACK, D], BF16, name="k_raw%d" % b)
+            nc.sync.dma_start(out=k_raw[b][:], in_=k[b].rearrange("(p j) d -> p j d", j=PACK))
+            for h in range(HALVES):
+                rows = slice(h * ROWS * P, (h + 1) * ROWS * P)
+                q_raw[(b, h)] = keep.tile([P, ROWS, D], BF16, name="q_raw%d%d" % (b, h))
+                nc.sync.dma_start(
+                    out=q_raw[(b, h)][:],
+                    in_=q[b, rows, :].rearrange("(p r) d -> p r d", r=ROWS),
+                )
+
+        identity = keep.tile([P, P], F32)
+        make_identity(nc, identity[:])
+
+        v_grouped = keep.tile([P, B, E, PACK], BF16, align_bytes=64)
+        v_codes = keep.tile([P, B * E], U32, align_bytes=64)
+        v_scales = keep.tile([P, B * E], U8, align_bytes=64)
+        nc.vector.tensor_copy(out=v_grouped[:], in_=v_raw[:].rearrange("p b j e -> p b e j"))
+        nc.vector.quantize_mx(
+            out=v_codes[:].bitcast(FP8X4),
+            scales=v_scales[:],
+            in_=v_grouped[:].rearrange("p b e j -> p (b e j)"),
+        )
+
+        qt_psum = {}
+        kv_psum = {}
+        for b in range(B):
+            for h in range(HALVES):
+                q_words = q_raw[(b, h)][:].rearrange("p r d -> p (r d)").bitcast(F32)
+                qt_psum[(b, h)] = qt_banks.tile([P, 2 * ROWS * P], F32, name="qt_psum")
+                for u in range(2):
+                    for r in range(ROWS):
+                        block = u * ROWS + r
+                        first_word = r * PAIRS + u
+                        nc.tensor.transpose(
+                            qt_psum[(b, h)][:, block * P : (block + 1) * P],
+                            q_words[:, first_word : (r + 1) * PAIRS : 2],
+                            identity[:],
+                        )
+
+            k_grouped = keep.tile([P, D, PACK], BF16, name="k_grouped%d" % b, align_bytes=64)
+            k_source = k_raw[b][:].rearrange("p j (m t) -> p t m j", t=PACK)
+            k_target = k_grouped[:].rearrange("p (t m) j -> p t m j", t=PACK)
+            split = K_GROUPS_ON_VECTOR if b == 0 else P
+            nc.vector.tensor_scalar_mul(
+                out=k_target[:, :, :split], in0=k_source[:, :, :split], scalar1=SCALE
+            )
+            if split < P:
+                nc.scalar.mul(out=k_target[:, :, split:], in_=k_source[:, :, split:], mul=SCALE)
+
+            k_codes = keep.tile([P, D], U32, name="k_codes%d" % b, align_bytes=64)
+            k_scales = keep.tile([P, D], U8, name="k_scales%d" % b, align_bytes=64)
+            nc.vector.quantize_mx(
+                out=k_codes[:].bitcast(FP8X4),
+                scales=k_scales[:],
+                in_=k_grouped[:].rearrange("p c j -> p (c j)"),
+            )
+
+            kv_psum[b] = kv_banks.tile([P, PACK, E], F32, name="kv_psum")
+            value_cols = slice(b * E, (b + 1) * E)
+            for i in range(PACK):
+                feature_cols = slice(i * P, (i + 1) * P)
+                nc.tensor.matmul_mx(
+                    out=kv_psum[b][:, i, :],
+                    lhsT=k_codes[:, feature_cols].bitcast(FP8X4),
+                    lhsT_scale=k_scales[:, feature_cols],
+                    rhs=v_codes[:, value_cols].bitcast(FP8X4),
+                    rhs_scale=v_scales[:, value_cols],
+                    start=True,
+                    stop=True,
+                )
+
+        q_codes = {}
+        q_scales = {}
+        kv_codes = {}
+        kv_scales = {}
+        for b in range(B):
+            q_grouped = {}
+            for h in range(HALVES):
+                q_grouped[h] = keep.tile(
+                    [P, ROWS * P, PACK], BF16, name="q_grouped%d%d" % (b, h), align_bytes=64
+                )
+                q_source = (
+                    qt_psum[(b, h)][:].bitcast(BF16).rearrange("p (u m e) -> p m u e", u=2, e=2)
+                )
+                q_target = q_grouped[h][:].rearrange("p m (u e) -> p m u e", e=2)
+                if (b, h) == (B - 1, HALVES - 1):
+                    nc.vector.tensor_scalar_mul(out=q_target, in0=q_source, scalar1=SCALE)
+                else:
+                    nc.scalar.mul(out=q_target, in_=q_source, mul=SCALE)
+
+            kv_grouped = keep.tile([P, E, PACK], BF16, name="kv_grouped%d" % b, align_bytes=64)
+            nc.scalar.copy(
+                out=kv_grouped[:], in_=kv_psum[b][:].rearrange("p t n -> p n t")
+            )
+
+            for h in range(HALVES):
+                q_codes[(b, h)] = keep.tile(
+                    [P, ROWS * P], U32, name="q_codes%d%d" % (b, h), align_bytes=64
+                )
+                q_scales[(b, h)] = keep.tile(
+                    [P, ROWS * P], U8, name="q_scales%d%d" % (b, h), align_bytes=64
+                )
+                nc.vector.quantize_mx(
+                    out=q_codes[(b, h)][:].bitcast(FP8X4),
+                    scales=q_scales[(b, h)][:],
+                    in_=q_grouped[h][:].rearrange("p m t -> p (m t)"),
+                )
+            kv_codes[b] = keep.tile([P, E], U32, name="kv_codes%d" % b, align_bytes=64)
+            kv_scales[b] = keep.tile([P, E], U8, name="kv_scales%d" % b, align_bytes=64)
+            nc.vector.quantize_mx(
+                out=kv_codes[b][:].bitcast(FP8X4),
+                scales=kv_scales[b][:],
+                in_=kv_grouped[:].rearrange("p n t -> p (n t)"),
+            )
+
+        for b in range(B):
+            for h in range(HALVES):
+                out_psum = out_banks.tile([P, ROWS, E], F32, name="out_psum")
+                for r in range(ROWS):
+                    row_cols = slice(r * P, (r + 1) * P)
+                    nc.tensor.matmul_mx(
+                        out=out_psum[:, r, :],
+                        lhsT=q_codes[(b, h)][:, row_cols].bitcast(FP8X4),
+                        lhsT_scale=q_scales[(b, h)][:, row_cols],
+                        rhs=kv_codes[b][:].bitcast(FP8X4),
+                        rhs_scale=kv_scales[b][:],
+                        start=True,
+                        stop=True,
+                    )
+                out_sbuf = keep.tile([P, ROWS, E], F32, name="out_sbuf%d%d" % (b, h))
+                if h % 2 == 0:
+                    nc.scalar.copy(out=out_sbuf[:], in_=out_psum[:])
+                else:
+                    nc.vector.tensor_copy(out=out_sbuf[:], in_=out_psum[:])
+                rows = slice(h * ROWS * P, (h + 1) * ROWS * P)
+                nc.sync.dma_start(
+                    out=out[b, rows, :].rearrange("(p r) e -> p r e", r=ROWS), in_=out_sbuf[:]
+                )

@@ -20,32 +20,39 @@ ROWS = 2
 FLOPS = 2 * 2 * B * S * D * E
 SCALE = 1.0 / math.sqrt(S)
 
-K_GROUPS_ON_VECTOR = 84
+K_GROUPS_ON_VECTOR = (84, 64)
 
 
 def tile_efficientattention_s_kernel(tc, q, k, v, out):
     nc = tc.nc
     with ExitStack() as ctx:
         keep = ctx.enter_context(tc.tile_pool(name="keep", bufs=1))
-        qt_banks = ctx.enter_context(tc.psum_pool(name="qt_banks", bufs=B * HALVES))
-        kv_banks = ctx.enter_context(tc.psum_pool(name="kv_banks", bufs=B))
-        out_banks = ctx.enter_context(tc.psum_pool(name="out_banks", bufs=2))
+        banks = ctx.enter_context(tc.psum_pool(name="banks", bufs=8))
         ctx.enter_context(tc.manual_schedule())
 
         v_raw = keep.tile([P, B, PACK, E], BF16)
         nc.sync.dma_start(out=v_raw[:], in_=v.rearrange("b (p j) e -> p b j e", j=PACK))
         k_raw = {}
         q_raw = {}
-        for b in range(B):
+
+        def load_k(b):
             k_raw[b] = keep.tile([P, PACK, D], BF16, name="k_raw%d" % b)
             nc.sync.dma_start(out=k_raw[b][:], in_=k[b].rearrange("(p j) d -> p j d", j=PACK))
-            for h in range(HALVES):
-                rows = slice(h * ROWS * P, (h + 1) * ROWS * P)
-                q_raw[(b, h)] = keep.tile([P, ROWS, D], BF16, name="q_raw%d%d" % (b, h))
-                nc.sync.dma_start(
-                    out=q_raw[(b, h)][:],
-                    in_=q[b, rows, :].rearrange("(p r) d -> p r d", r=ROWS),
-                )
+
+        def load_q(b, h):
+            rows = slice(h * ROWS * P, (h + 1) * ROWS * P)
+            q_raw[(b, h)] = keep.tile([P, ROWS, D], BF16, name="q_raw%d%d" % (b, h))
+            nc.sync.dma_start(
+                out=q_raw[(b, h)][:],
+                in_=q[b, rows, :].rearrange("(p r) d -> p r d", r=ROWS),
+            )
+
+        load_k(0)
+        load_q(0, 0)
+        load_k(1)
+        load_q(0, 1)
+        load_q(1, 0)
+        load_q(1, 1)
 
         identity = keep.tile([P, P], F32)
         make_identity(nc, identity[:])
@@ -53,125 +60,206 @@ def tile_efficientattention_s_kernel(tc, q, k, v, out):
         v_grouped = keep.tile([P, B, E, PACK], BF16, align_bytes=64)
         v_codes = keep.tile([P, B * E], U32, align_bytes=64)
         v_scales = keep.tile([P, B * E], U8, align_bytes=64)
-        nc.vector.tensor_copy(out=v_grouped[:], in_=v_raw[:].rearrange("p b j e -> p b e j"))
-        nc.vector.quantize_mx(
-            out=v_codes[:].bitcast(FP8X4),
-            scales=v_scales[:],
-            in_=v_grouped[:].rearrange("p b e j -> p (b e j)"),
-        )
-
-        qt_psum = {}
+        k_grouped = {}
+        k_codes = {}
+        k_scales = {}
         kv_psum = {}
+        kv_grouped = {}
+        kv_codes = {}
+        kv_scales = {}
         for b in range(B):
-            for h in range(HALVES):
-                q_words = q_raw[(b, h)][:].rearrange("p r d -> p (r d)").bitcast(F32)
-                qt_psum[(b, h)] = qt_banks.tile([P, 2 * ROWS * P], F32, name="qt_psum")
-                for u in range(2):
-                    for r in range(ROWS):
-                        block = u * ROWS + r
-                        first_word = r * PAIRS + u
-                        nc.tensor.transpose(
-                            qt_psum[(b, h)][:, block * P : (block + 1) * P],
-                            q_words[:, first_word : (r + 1) * PAIRS : 2],
-                            identity[:],
-                        )
-
-            k_grouped = keep.tile([P, D, PACK], BF16, name="k_grouped%d" % b, align_bytes=64)
-            k_source = k_raw[b][:].rearrange("p j (m t) -> p t m j", t=PACK)
-            k_target = k_grouped[:].rearrange("p (t m) j -> p t m j", t=PACK)
-            split = K_GROUPS_ON_VECTOR if b == 0 else P
-            nc.vector.tensor_scalar_mul(
-                out=k_target[:, :, :split], in0=k_source[:, :, :split], scalar1=SCALE
+            k_grouped[b] = keep.tile([P, D, PACK], BF16, name="k_grouped%d" % b, align_bytes=64)
+            k_codes[b] = keep.tile([P, D], U32, name="k_codes%d" % b, align_bytes=64)
+            k_scales[b] = keep.tile([P, D], U8, name="k_scales%d" % b, align_bytes=64)
+            kv_psum[b] = banks.tile([P, PACK * E], F32, name="bank")
+            kv_grouped[b] = keep.tile([P, E, PACK], BF16, name="kv_grouped%d" % b, align_bytes=64)
+            kv_codes[b] = keep.tile([P, E], U32, name="kv_codes%d" % b, align_bytes=64)
+            kv_scales[b] = keep.tile([P, E], U8, name="kv_scales%d" % b, align_bytes=64)
+        qt_psum = {}
+        q_grouped = {}
+        q_codes = {}
+        q_scales = {}
+        for bh in q_raw:
+            qt_psum[bh] = banks.tile([P, 2 * ROWS * P], F32, name="bank")
+            q_grouped[bh] = keep.tile(
+                [P, ROWS * P, PACK], BF16, name="q_grouped%d%d" % bh, align_bytes=64
             )
-            if split < P:
-                nc.scalar.mul(out=k_target[:, :, split:], in_=k_source[:, :, split:], mul=SCALE)
+            q_codes[bh] = keep.tile([P, ROWS * P], U32, name="q_codes%d%d" % bh, align_bytes=64)
+            q_scales[bh] = keep.tile([P, ROWS * P], U8, name="q_scales%d%d" % bh, align_bytes=64)
 
-            k_codes = keep.tile([P, D], U32, name="k_codes%d" % b, align_bytes=64)
-            k_scales = keep.tile([P, D], U8, name="k_scales%d" % b, align_bytes=64)
+        def quantise(codes, scales, grouped, cols):
             nc.vector.quantize_mx(
-                out=k_codes[:].bitcast(FP8X4),
-                scales=k_scales[:],
-                in_=k_grouped[:].rearrange("p c j -> p (c j)"),
+                out=codes[:, cols].bitcast(FP8X4),
+                scales=scales[:, cols],
+                in_=grouped[:, cols.start * PACK : cols.stop * PACK],
             )
 
-            kv_psum[b] = kv_banks.tile([P, PACK, E], F32, name="kv_psum")
+        def group_v(b):
+            nc.vector.tensor_copy(
+                out=v_grouped[:, b], in_=v_raw[:, b].rearrange("p j e -> p e j")
+            )
+
+        def quantise_v(b):
+            quantise(
+                v_codes,
+                v_scales,
+                v_grouped[:].rearrange("p b e j -> p (b e j)"),
+                slice(b * E, (b + 1) * E),
+            )
+
+        def group_k(b, half):
+            runs = slice(2 * half, 2 * half + 2)
+            source = k_raw[b][:].rearrange("p j (m t) -> p t m j", t=PACK)[:, runs]
+            target = k_grouped[b][:].rearrange("p (t m) j -> p t m j", t=PACK)[:, runs]
+            split = K_GROUPS_ON_VECTOR[b]
+            nc.scalar.mul(out=target[:, :, split:], in_=source[:, :, split:], mul=SCALE)
+            nc.vector.tensor_scalar_mul(
+                out=target[:, :, :split], in0=source[:, :, :split], scalar1=SCALE
+            )
+
+        def quantise_k(b, half):
+            quantise(
+                k_codes[b],
+                k_scales[b],
+                k_grouped[b][:].rearrange("p c j -> p (c j)"),
+                slice(half * D // 2, (half + 1) * D // 2),
+            )
+
+        def multiply_kv(b):
             value_cols = slice(b * E, (b + 1) * E)
-            for i in range(PACK):
-                feature_cols = slice(i * P, (i + 1) * P)
+            for t in range(PACK):
+                feature_cols = slice(t * P, (t + 1) * P)
                 nc.tensor.matmul_mx(
-                    out=kv_psum[b][:, i, :],
-                    lhsT=k_codes[:, feature_cols].bitcast(FP8X4),
-                    lhsT_scale=k_scales[:, feature_cols],
+                    out=kv_psum[b][:, t * E : (t + 1) * E],
+                    lhsT=k_codes[b][:, feature_cols].bitcast(FP8X4),
+                    lhsT_scale=k_scales[b][:, feature_cols],
                     rhs=v_codes[:, value_cols].bitcast(FP8X4),
                     rhs_scale=v_scales[:, value_cols],
                     start=True,
                     stop=True,
                 )
 
-        q_codes = {}
-        q_scales = {}
-        kv_codes = {}
-        kv_scales = {}
-        for b in range(B):
-            q_grouped = {}
-            for h in range(HALVES):
-                q_grouped[h] = keep.tile(
-                    [P, ROWS * P, PACK], BF16, name="q_grouped%d%d" % (b, h), align_bytes=64
-                )
-                q_source = (
-                    qt_psum[(b, h)][:].bitcast(BF16).rearrange("p (u m e) -> p m u e", u=2, e=2)
-                )
-                q_target = q_grouped[h][:].rearrange("p m (u e) -> p m u e", e=2)
-                if (b, h) == (B - 1, HALVES - 1):
-                    nc.vector.tensor_scalar_mul(out=q_target, in0=q_source, scalar1=SCALE)
-                else:
-                    nc.scalar.mul(out=q_target, in_=q_source, mul=SCALE)
+        def copy_kv(b, copy):
+            copy(out=kv_grouped[b][:], in_=kv_psum[b][:].rearrange("p (t n) -> p n t", t=PACK))
 
-            kv_grouped = keep.tile([P, E, PACK], BF16, name="kv_grouped%d" % b, align_bytes=64)
-            nc.scalar.copy(
-                out=kv_grouped[:], in_=kv_psum[b][:].rearrange("p t n -> p n t")
+        def quantise_kv(b):
+            quantise(
+                kv_codes[b],
+                kv_scales[b],
+                kv_grouped[b][:].rearrange("p n t -> p (n t)"),
+                slice(0, E),
             )
 
-            for h in range(HALVES):
-                q_codes[(b, h)] = keep.tile(
-                    [P, ROWS * P], U32, name="q_codes%d%d" % (b, h), align_bytes=64
-                )
-                q_scales[(b, h)] = keep.tile(
-                    [P, ROWS * P], U8, name="q_scales%d%d" % (b, h), align_bytes=64
-                )
-                nc.vector.quantize_mx(
-                    out=q_codes[(b, h)][:].bitcast(FP8X4),
-                    scales=q_scales[(b, h)][:],
-                    in_=q_grouped[h][:].rearrange("p m t -> p (m t)"),
-                )
-            kv_codes[b] = keep.tile([P, E], U32, name="kv_codes%d" % b, align_bytes=64)
-            kv_scales[b] = keep.tile([P, E], U8, name="kv_scales%d" % b, align_bytes=64)
-            nc.vector.quantize_mx(
-                out=kv_codes[b][:].bitcast(FP8X4),
-                scales=kv_scales[b][:],
-                in_=kv_grouped[:].rearrange("p n t -> p (n t)"),
-            )
-
-        for b in range(B):
-            for h in range(HALVES):
-                out_psum = out_banks.tile([P, ROWS, E], F32, name="out_psum")
+        def transpose_q(b, h):
+            words = q_raw[(b, h)][:].rearrange("p r d -> p (r d)").bitcast(F32)
+            for u in range(2):
                 for r in range(ROWS):
-                    row_cols = slice(r * P, (r + 1) * P)
-                    nc.tensor.matmul_mx(
-                        out=out_psum[:, r, :],
-                        lhsT=q_codes[(b, h)][:, row_cols].bitcast(FP8X4),
-                        lhsT_scale=q_scales[(b, h)][:, row_cols],
-                        rhs=kv_codes[b][:].bitcast(FP8X4),
-                        rhs_scale=kv_scales[b][:],
-                        start=True,
-                        stop=True,
+                    block = u * ROWS + r
+                    nc.tensor.transpose(
+                        qt_psum[(b, h)][:, block * P : (block + 1) * P],
+                        words[:, r * PAIRS + u : (r + 1) * PAIRS : 2],
+                        identity[:],
                     )
-                out_sbuf = keep.tile([P, ROWS, E], F32, name="out_sbuf%d%d" % (b, h))
-                if h % 2 == 0:
-                    nc.scalar.copy(out=out_sbuf[:], in_=out_psum[:])
-                else:
-                    nc.vector.tensor_copy(out=out_sbuf[:], in_=out_psum[:])
-                rows = slice(h * ROWS * P, (h + 1) * ROWS * P)
-                nc.sync.dma_start(
-                    out=out[b, rows, :].rearrange("(p r) e -> p r e", r=ROWS), in_=out_sbuf[:]
+
+        def q_views(b, h):
+            source = (
+                qt_psum[(b, h)][:].bitcast(BF16).rearrange("p (u m e) -> p m u e", u=2, e=2)
+            )
+            target = q_grouped[(b, h)][:].rearrange("p m (u e) -> p m u e", e=2)
+            return source, target
+
+        def scale_q_on_scalar(b, h):
+            source, target = q_views(b, h)
+            nc.scalar.mul(out=target, in_=source, mul=SCALE)
+
+        def scale_q_on_vector(b, h):
+            source, target = q_views(b, h)
+            nc.vector.tensor_scalar_mul(out=target, in0=source, scalar1=SCALE)
+
+        def quantise_q(b, h):
+            quantise(
+                q_codes[(b, h)],
+                q_scales[(b, h)],
+                q_grouped[(b, h)][:].rearrange("p m t -> p (m t)"),
+                slice(0, ROWS * P),
+            )
+
+        out_psum = {}
+
+        def multiply_out(b, h):
+            last = (b, h) == (B - 1, HALVES - 1)
+            for r in range(ROWS):
+                if last or r == 0:
+                    bank = banks.tile([P, PACK * E], F32, name="bank")
+                first_col = 0 if last else r * E
+                out_psum[(b, h, r)] = bank[:, first_col : first_col + E]
+                row_cols = slice(r * P, (r + 1) * P)
+                nc.tensor.matmul_mx(
+                    out=out_psum[(b, h, r)],
+                    lhsT=q_codes[(b, h)][:, row_cols].bitcast(FP8X4),
+                    lhsT_scale=q_scales[(b, h)][:, row_cols],
+                    rhs=kv_codes[b][:].bitcast(FP8X4),
+                    rhs_scale=kv_scales[b][:],
+                    start=True,
+                    stop=True,
                 )
+            if not last:
+                out_psum[(b, h)] = bank[:, : ROWS * E]
+
+        def store(b, h):
+            rows = slice(h * ROWS * P, (h + 1) * ROWS * P)
+            nc.sync.dma_start(
+                out=out[b, rows, :].rearrange("(p r) e -> p r e", r=ROWS), in_=out_sbuf[(b, h)][:]
+            )
+
+        out_sbuf = {}
+        for bh in q_raw:
+            out_sbuf[bh] = keep.tile([P, ROWS, E], F32, name="out_sbuf%d%d" % bh)
+
+        def copy_out(b, h, copy):
+            copy(
+                out=out_sbuf[(b, h)][:].rearrange("p r e -> p (r e)"),
+                in_=out_psum[(b, h)],
+            )
+            store(b, h)
+
+        group_v(0)
+        group_v(1)
+        quantise_v(0)
+        quantise_v(1)
+        group_k(0, 0)
+        group_k(0, 1)
+        quantise_k(0, 0)
+        quantise_k(0, 1)
+        transpose_q(0, 0)
+        multiply_kv(0)
+        scale_q_on_vector(0, 0)
+        group_k(1, 0)
+        group_k(1, 1)
+        transpose_q(0, 1)
+        transpose_q(1, 0)
+        quantise_q(0, 0)
+        quantise_k(1, 0)
+        quantise_k(1, 1)
+        copy_kv(0, nc.scalar.copy)
+        multiply_kv(1)
+        transpose_q(1, 1)
+        scale_q_on_scalar(0, 1)
+        quantise_kv(0)
+        scale_q_on_vector(1, 0)
+        multiply_out(0, 0)
+        quantise_q(0, 1)
+        copy_kv(1, nc.scalar.copy)
+        scale_q_on_vector(1, 1)
+        quantise_q(1, 0)
+        multiply_out(0, 1)
+        quantise_kv(1)
+        quantise_q(1, 1)
+        multiply_out(1, 0)
+        multiply_out(1, 1)
+        copy_out(0, 0, nc.scalar.copy)
+        copy_out(0, 1, nc.scalar.copy)
+        copy_out(1, 0, nc.vector.tensor_copy)
+        nc.vector.tensor_copy(out=out_sbuf[(1, 1)][:, 0, :], in_=out_psum[(1, 1, 0)])
+        nc.scalar.copy(out=out_sbuf[(1, 1)][:, 1, :], in_=out_psum[(1, 1, 1)])
+        store(1, 1)

@@ -96,7 +96,8 @@ def tile_efficientattention_s_kernel(tc, q, k, v, out):
 
         def group_v(b):
             nc.vector.tensor_copy(
-                out=v_grouped[:, b], in_=v_raw[:, b].rearrange("p j e -> p e j")
+                out=v_grouped[:, b].rearrange("p (c i) j -> p c j i", i=PACK),
+                in_=v_raw[:, b].rearrange("p j (c i) -> p c j i", i=PACK),
             )
 
         def quantise_v(b):
@@ -109,12 +110,12 @@ def tile_efficientattention_s_kernel(tc, q, k, v, out):
 
         def group_k(b, half):
             runs = slice(2 * half, 2 * half + 2)
-            source = k_raw[b][:].rearrange("p j (m t) -> p t m j", t=PACK)[:, runs]
-            target = k_grouped[b][:].rearrange("p (t m) j -> p t m j", t=PACK)[:, runs]
+            source = k_raw[b][:].rearrange("p j (m t) -> p m j t", t=PACK)[:, :, :, runs]
+            target = k_grouped[b][:].rearrange("p (t m) j -> p m j t", t=PACK)[:, :, :, runs]
             split = K_GROUPS_ON_VECTOR[b]
-            nc.scalar.mul(out=target[:, :, split:], in_=source[:, :, split:], mul=SCALE)
+            nc.scalar.mul(out=target[:, split:], in_=source[:, split:], mul=SCALE)
             nc.vector.tensor_scalar_mul(
-                out=target[:, :, :split], in0=source[:, :, :split], scalar1=SCALE
+                out=target[:, :split], in0=source[:, :split], scalar1=SCALE
             )
 
         def quantise_k(b, half):

@@ -17,6 +17,8 @@ PAIRS = D // 2
 HALVES = 2
 ROWS = 2
 
+BANK = 512
+
 FLOPS = 2 * 2 * B * S * D * E
 SCALE = 1.0 / math.sqrt(S)
 
@@ -30,10 +32,16 @@ def tile_efficientattention_s_kernel(tc, q, k, v, out):
         banks = ctx.enter_context(tc.psum_pool(name="banks", bufs=8))
         ctx.enter_context(tc.manual_schedule())
 
+        def new_bank():
+            bank = banks.tile([P, BANK], F32, name="bank")
+            return bank
+
         v_raw = keep.tile([P, B, PACK, E], BF16)
-        nc.sync.dma_start(out=v_raw[:], in_=v.rearrange("b (p j) e -> p b j e", j=PACK))
         k_raw = {}
         q_raw = {}
+
+        def load_v():
+            nc.sync.dma_start(out=v_raw[:], in_=v.rearrange("b (p j) e -> p b j e", j=PACK))
 
         def load_k(b):
             k_raw[b] = keep.tile([P, PACK, D], BF16, name="k_raw%d" % b)
@@ -47,6 +55,7 @@ def tile_efficientattention_s_kernel(tc, q, k, v, out):
                 in_=q[b, rows, :].rearrange("(p r) d -> p r d", r=ROWS),
             )
 
+        load_v()
         load_k(0)
         load_q(0, 0)
         load_k(1)
@@ -71,21 +80,21 @@ def tile_efficientattention_s_kernel(tc, q, k, v, out):
             k_grouped[b] = keep.tile([P, D, PACK], BF16, name="k_grouped%d" % b, align_bytes=64)
             k_codes[b] = keep.tile([P, D], U32, name="k_codes%d" % b, align_bytes=64)
             k_scales[b] = keep.tile([P, D], U8, name="k_scales%d" % b, align_bytes=64)
-            kv_psum[b] = banks.tile([P, PACK * E], F32, name="bank")
+            kv_psum[b] = new_bank()
             kv_grouped[b] = keep.tile([P, E, PACK], BF16, name="kv_grouped%d" % b, align_bytes=64)
             kv_codes[b] = keep.tile([P, E], U32, name="kv_codes%d" % b, align_bytes=64)
             kv_scales[b] = keep.tile([P, E], U8, name="kv_scales%d" % b, align_bytes=64)
-        qt_psum = {}
         q_grouped = {}
         q_codes = {}
         q_scales = {}
+        out_sbuf = {}
         for bh in q_raw:
-            qt_psum[bh] = banks.tile([P, 2 * ROWS * P], F32, name="bank")
             q_grouped[bh] = keep.tile(
                 [P, ROWS * P, PACK], BF16, name="q_grouped%d%d" % bh, align_bytes=64
             )
             q_codes[bh] = keep.tile([P, ROWS * P], U32, name="q_codes%d%d" % bh, align_bytes=64)
             q_scales[bh] = keep.tile([P, ROWS * P], U8, name="q_scales%d%d" % bh, align_bytes=64)
+            out_sbuf[bh] = keep.tile([P, ROWS * E], F32, name="out_sbuf%d%d" % bh)
 
         def quantise(codes, scales, grouped, cols):
             nc.vector.quantize_mx(
@@ -151,52 +160,50 @@ def tile_efficientattention_s_kernel(tc, q, k, v, out):
                 slice(0, E),
             )
 
-        def transpose_q(b, h):
+        qt_psum = {}
+        out_psum = {}
+
+        def transpose_q(piece):
+            b, h, first, count = piece
             words = q_raw[(b, h)][:].rearrange("p r d -> p (r d)").bitcast(F32)
-            for u in range(2):
-                for r in range(ROWS):
-                    block = u * ROWS + r
+            bank = new_bank()
+            qt_psum[piece] = bank
+            for i in range(count):
+                for u in range(2):
+                    block = u * count + i
                     nc.tensor.transpose(
-                        qt_psum[(b, h)][:, block * P : (block + 1) * P],
-                        words[:, r * PAIRS + u : (r + 1) * PAIRS : 2],
+                        bank[:, block * P : (block + 1) * P],
+                        words[:, (first + i) * PAIRS + u : (first + i + 1) * PAIRS : 2],
                         identity[:],
                     )
 
-        def q_views(b, h):
-            source = (
-                qt_psum[(b, h)][:].bitcast(BF16).rearrange("p (u m e) -> p m u e", u=2, e=2)
+        def scale_q(piece, multiply):
+            b, h, first, count = piece
+            source = qt_psum[piece][:, : count * PAIRS].bitcast(BF16)
+            target = q_grouped[(b, h)][:, first * P : (first + count) * P, :]
+            multiply(
+                target.rearrange("p m (u e) -> p m u e", e=2),
+                source.rearrange("p (u m e) -> p m u e", u=2, e=2),
+                SCALE,
             )
-            target = q_grouped[(b, h)][:].rearrange("p m (u e) -> p m u e", e=2)
-            return source, target
 
-        def scale_q_on_scalar(b, h):
-            source, target = q_views(b, h)
-            nc.scalar.mul(out=target, in_=source, mul=SCALE)
-
-        def scale_q_on_vector(b, h):
-            source, target = q_views(b, h)
-            nc.vector.tensor_scalar_mul(out=target, in0=source, scalar1=SCALE)
-
-        def quantise_q(b, h):
+        def quantise_q(piece):
+            b, h, first, count = piece
             quantise(
                 q_codes[(b, h)],
                 q_scales[(b, h)],
                 q_grouped[(b, h)][:].rearrange("p m t -> p (m t)"),
-                slice(0, ROWS * P),
+                slice(first * P, (first + count) * P),
             )
 
-        out_psum = {}
-
-        def multiply_out(b, h):
-            last = (b, h) == (B - 1, HALVES - 1)
-            for r in range(ROWS):
-                if last or r == 0:
-                    bank = banks.tile([P, PACK * E], F32, name="bank")
-                first_col = 0 if last else r * E
-                out_psum[(b, h, r)] = bank[:, first_col : first_col + E]
-                row_cols = slice(r * P, (r + 1) * P)
+        def multiply_out(piece):
+            b, h, first, count = piece
+            bank = new_bank()
+            out_psum[piece] = bank
+            for i in range(count):
+                row_cols = slice((first + i) * P, (first + i + 1) * P)
                 nc.tensor.matmul_mx(
-                    out=out_psum[(b, h, r)],
+                    out=bank[:, i * E : (i + 1) * E],
                     lhsT=q_codes[(b, h)][:, row_cols].bitcast(FP8X4),
                     lhsT_scale=q_scales[(b, h)][:, row_cols],
                     rhs=kv_codes[b][:].bitcast(FP8X4),
@@ -204,25 +211,28 @@ def tile_efficientattention_s_kernel(tc, q, k, v, out):
                     start=True,
                     stop=True,
                 )
-            if not last:
-                out_psum[(b, h)] = bank[:, : ROWS * E]
+
+        def copy_out(piece, copy):
+            b, h, first, count = piece
+            copy(
+                out=out_sbuf[(b, h)][:, first * E : (first + count) * E],
+                in_=out_psum[piece][:, : count * E],
+            )
 
         def store(b, h):
             rows = slice(h * ROWS * P, (h + 1) * ROWS * P)
             nc.sync.dma_start(
-                out=out[b, rows, :].rearrange("(p r) e -> p r e", r=ROWS), in_=out_sbuf[(b, h)][:]
+                out=out[b, rows, :].rearrange("(p r) e -> p (r e)", r=ROWS),
+                in_=out_sbuf[(b, h)][:],
             )
 
-        out_sbuf = {}
-        for bh in q_raw:
-            out_sbuf[bh] = keep.tile([P, ROWS, E], F32, name="out_sbuf%d%d" % bh)
-
-        def copy_out(b, h, copy):
-            copy(
-                out=out_sbuf[(b, h)][:].rearrange("p r e -> p (r e)"),
-                in_=out_psum[(b, h)],
-            )
-            store(b, h)
+        on_scalar = nc.scalar.mul
+        on_vector = nc.vector.tensor_scalar_mul
+        q00 = (0, 0, 0, 2)
+        q01 = (0, 1, 0, 2)
+        q10 = (1, 0, 0, 2)
+        q11a = (1, 1, 0, 1)
+        q11b = (1, 1, 1, 1)
 
         group_v(0)
         group_v(1)
@@ -232,35 +242,42 @@ def tile_efficientattention_s_kernel(tc, q, k, v, out):
         group_k(0, 1)
         quantise_k(0, 0)
         quantise_k(0, 1)
-        transpose_q(0, 0)
+        transpose_q(q00)
         multiply_kv(0)
-        scale_q_on_vector(0, 0)
+        scale_q(q00, on_vector)
         group_k(1, 0)
         group_k(1, 1)
-        transpose_q(0, 1)
-        transpose_q(1, 0)
-        quantise_q(0, 0)
+        transpose_q(q01)
+        transpose_q(q10)
+        quantise_q(q00)
         quantise_k(1, 0)
         quantise_k(1, 1)
         copy_kv(0, nc.scalar.copy)
         multiply_kv(1)
-        transpose_q(1, 1)
-        scale_q_on_scalar(0, 1)
+        transpose_q(q11a)
+        transpose_q(q11b)
+        scale_q(q01, on_scalar)
         quantise_kv(0)
-        scale_q_on_vector(1, 0)
-        multiply_out(0, 0)
-        quantise_q(0, 1)
+        scale_q(q10, on_vector)
+        multiply_out(q00)
+        quantise_q(q01)
+        multiply_out(q01)
         copy_kv(1, nc.scalar.copy)
-        scale_q_on_vector(1, 1)
-        quantise_q(1, 0)
-        multiply_out(0, 1)
+        scale_q(q11a, on_vector)
+        scale_q(q11b, on_scalar)
+        quantise_q(q10)
         quantise_kv(1)
-        quantise_q(1, 1)
-        multiply_out(1, 0)
-        multiply_out(1, 1)
-        copy_out(0, 0, nc.scalar.copy)
-        copy_out(0, 1, nc.scalar.copy)
-        copy_out(1, 0, nc.vector.tensor_copy)
-        nc.vector.tensor_copy(out=out_sbuf[(1, 1)][:, 0, :], in_=out_psum[(1, 1, 0)])
-        nc.scalar.copy(out=out_sbuf[(1, 1)][:, 1, :], in_=out_psum[(1, 1, 1)])
+        quantise_q(q11a)
+        quantise_q(q11b)
+        multiply_out(q10)
+        multiply_out(q11a)
+        multiply_out(q11b)
+        copy_out(q00, nc.scalar.copy)
+        store(0, 0)
+        copy_out(q01, nc.scalar.copy)
+        store(0, 1)
+        copy_out(q10, nc.vector.tensor_copy)
+        store(1, 0)
+        copy_out(q11a, nc.scalar.copy)
+        copy_out(q11b, nc.vector.tensor_copy)
         store(1, 1)

@@ -24,6 +24,8 @@ SCALE = 1.0 / math.sqrt(S)
 
 K_GROUPS_ON_VECTOR = (84, 64)
 
+WARM_PASSES = 3
+
 
 def tile_efficientattention_s_kernel(tc, q, k, v, out):
     nc = tc.nc
@@ -228,12 +230,25 @@ def tile_efficientattention_s_kernel(tc, q, k, v, out):
 
         on_scalar = nc.scalar.mul
         on_vector = nc.vector.tensor_scalar_mul
+
+        def warm_tensor():
+            words = v_raw[:].rearrange("p b j e -> p (b j e)").bitcast(F32)
+            for i in range(WARM_PASSES):
+                nc.tensor.matmul(
+                    kv_psum[1][:, i * P : (i + 1) * P],
+                    identity[:],
+                    words[:, i * P : (i + 1) * P],
+                    start=True,
+                    stop=True,
+                )
+
         q00 = (0, 0, 0, 2)
         q01 = (0, 1, 0, 2)
         q10 = (1, 0, 0, 2)
         q11a = (1, 1, 0, 1)
         q11b = (1, 1, 1, 1)
 
+        warm_tensor()
         group_v(0)
         group_v(1)
         quantise_v(0)

@@ -22,7 +22,7 @@ BANK = 512
 FLOPS = 2 * 2 * B * S * D * E
 SCALE = 1.0 / math.sqrt(S)
 
-K_GROUPS_ON_VECTOR = (84, 64)
+K_GROUPS_ON_VECTOR = (84, 76)
 
 WARM_PASSES = 3
 

@@ -22,7 +22,7 @@ BANK = 512
 FLOPS = 2 * 2 * B * S * D * E
 SCALE = 1.0 / math.sqrt(S)
 
-K_GROUPS_ON_VECTOR = (84, 76)
+K_GROUPS_ON_VECTOR = (84, 68)
 
 WARM_PASSES = 3
 
@@ -119,8 +119,7 @@ def tile_efficientattention_s_kernel(tc, q, k, v, out):
                 slice(b * E, (b + 1) * E),
             )
 
-        def group_k(b, half):
-            runs = slice(2 * half, 2 * half + 2)
+        def group_k(b, runs):
             source = k_raw[b][:].rearrange("p j (m t) -> p m j t", t=PACK)[:, :, :, runs]
             target = k_grouped[b][:].rearrange("p (t m) j -> p m j t", t=PACK)[:, :, :, runs]
             split = K_GROUPS_ON_VECTOR[b]
@@ -253,15 +252,14 @@ def tile_efficientattention_s_kernel(tc, q, k, v, out):
         group_v(1)
         quantise_v(0)
         quantise_v(1)
-        group_k(0, 0)
-        group_k(0, 1)
+        group_k(0, slice(0, 2))
+        group_k(0, slice(2, 4))
         quantise_k(0, 0)
         quantise_k(0, 1)
         transpose_q(q00)
         multiply_kv(0)
         scale_q(q00, on_vector)
-        group_k(1, 0)
-        group_k(1, 1)
+        group_k(1, slice(0, 4))
         transpose_q(q01)
         transpose_q(q10)
         quantise_q(q00)

@@ -220,11 +220,14 @@ def tile_efficientattention_s_kernel(tc, q, k, v, out):
                 in_=out_psum[piece][:, : count * E],
             )
 
-        def store(b, h):
-            rows = slice(h * ROWS * P, (h + 1) * ROWS * P)
+        def store(piece):
+            b, h, first, count = piece
+            rows = out[b, h * ROWS * P : (h + 1) * ROWS * P, :]
             nc.sync.dma_start(
-                out=out[b, rows, :].rearrange("(p r) e -> p (r e)", r=ROWS),
-                in_=out_sbuf[(b, h)][:],
+                out=rows.rearrange("(p r) e -> p r e", r=ROWS)[:, first : first + count, :],
+                in_=out_sbuf[(b, h)][:, first * E : (first + count) * E].rearrange(
+                    "p (r e) -> p r e", r=count
+                ),
             )
 
         on_scalar = nc.scalar.mul
@@ -276,21 +279,22 @@ def tile_efficientattention_s_kernel(tc, q, k, v, out):
         quantise_q(q01)
         multiply_out(q01)
         copy_kv(1, nc.scalar.copy)
-        scale_q(q11a, on_vector)
-        scale_q(q11b, on_scalar)
+        scale_q(q11a, on_scalar)
         quantise_q(q10)
         quantise_kv(1)
-        quantise_q(q11a)
-        quantise_q(q11b)
+        scale_q(q11b, on_vector)
         multiply_out(q10)
+        quantise_q(q11a)
         multiply_out(q11a)
+        quantise_q(q11b)
         multiply_out(q11b)
         copy_out(q00, nc.scalar.copy)
-        store(0, 0)
+        store(q00)
         copy_out(q01, nc.scalar.copy)
-        store(0, 1)
-        copy_out(q10, nc.vector.tensor_copy)
-        store(1, 0)
-        copy_out(q11a, nc.scalar.copy)
+        store(q01)
+        copy_out(q10, nc.scalar.copy)
+        store(q10)
+        copy_out(q11a, nc.vector.tensor_copy)
+        store(q11a)
         copy_out(q11b, nc.vector.tensor_copy)
-        store(1, 1)
+        store(q11b)

@@ -107,8 +107,8 @@ def tile_efficientattention_s_kernel(tc, q, k, v, out):
 
         def group_v(b):
             nc.vector.tensor_copy(
-                out=v_grouped[:, b].rearrange("p (c i) j -> p c j i", i=PACK),
-                in_=v_raw[:, b].rearrange("p j (c i) -> p c j i", i=PACK),
+                out=v_grouped[:, b].rearrange("p (c i) j -> p c j i", i=8),
+                in_=v_raw[:, b].rearrange("p j (c i) -> p c j i", i=8),
             )
 
         def quantise_v(b):
@@ -151,7 +151,10 @@ def tile_efficientattention_s_kernel(tc, q, k, v, out):
                 )
 
         def copy_kv(b, copy):
-            copy(out=kv_grouped[b][:], in_=kv_psum[b][:].rearrange("p (t n) -> p n t", t=PACK))
+            copy(
+                out=kv_grouped[b][:].rearrange("p (c i) t -> p c t i", i=2),
+                in_=kv_psum[b][:].rearrange("p (t c i) -> p c t i", t=PACK, i=2),
+            )
 
         def quantise_kv(b):
             quantise(

@@ -22,7 +22,7 @@ BANK = 512
 FLOPS = 2 * 2 * B * S * D * E
 SCALE = 1.0 / math.sqrt(S)
 
-K_GROUPS_ON_VECTOR = (84, 68)
+K_GROUPS_ON_VECTOR = (84, 80)
 
 WARM_PASSES = 3
 
@@ -82,7 +82,6 @@ def tile_efficientattention_s_kernel(tc, q, k, v, out):
             k_grouped[b] = keep.tile([P, D, PACK], BF16, name="k_grouped%d" % b, align_bytes=64)
             k_codes[b] = keep.tile([P, D], U32, name="k_codes%d" % b, align_bytes=64)
             k_scales[b] = keep.tile([P, D], U8, name="k_scales%d" % b, align_bytes=64)
-            kv_psum[b] = new_bank()
             kv_grouped[b] = keep.tile([P, E, PACK], BF16, name="kv_grouped%d" % b, align_bytes=64)
             kv_codes[b] = keep.tile([P, E], U32, name="kv_codes%d" % b, align_bytes=64)
             kv_scales[b] = keep.tile([P, E], U8, name="kv_scales%d" % b, align_bytes=64)
@@ -137,6 +136,7 @@ def tile_efficientattention_s_kernel(tc, q, k, v, out):
             )
 
         def multiply_kv(b):
+            kv_psum[b] = new_bank()
             value_cols = slice(b * E, (b + 1) * E)
             for t in range(PACK):
                 feature_cols = slice(t * P, (t + 1) * P)
@@ -237,17 +237,19 @@ def tile_efficientattention_s_kernel(tc, q, k, v, out):
         on_vector = nc.vector.tensor_scalar_mul
 
         def warm_tensor():
-            words = v_raw[:].rearrange("p b j e -> p (b j e)").bitcast(F32)
+            bank = new_bank()
             for i in range(WARM_PASSES):
                 nc.tensor.matmul(
-                    kv_psum[1][:, i * P : (i + 1) * P],
+                    bank[:, i * P : (i + 1) * P],
                     identity[:],
-                    words[:, i * P : (i + 1) * P],
+                    identity[:],
                     start=True,
                     stop=True,
                 )
 
         q00 = (0, 0, 0, 2)
+        q00a = (0, 0, 0, 1)
+        q00b = (0, 0, 1, 1)
         q01 = (0, 1, 0, 2)
         q10 = (1, 0, 0, 2)
         q11a = (1, 1, 0, 1)
@@ -262,9 +264,11 @@ def tile_efficientattention_s_kernel(tc, q, k, v, out):
         group_k(0, slice(2, 4))
         quantise_k(0, 0)
         quantise_k(0, 1)
-        transpose_q(q00)
+        transpose_q(q00a)
+        transpose_q(q00b)
         multiply_kv(0)
-        scale_q(q00, on_vector)
+        scale_q(q00a, on_scalar)
+        scale_q(q00b, on_vector)
         group_k(1, slice(0, 4))
         transpose_q(q01)
         transpose_q(q10)

import math
from contextlib import ExitStack

import concourse.mybir as mybir
from concourse.masks import make_identity

BF16 = mybir.dt.bfloat16
F32 = mybir.dt.float32
U32 = mybir.dt.uint32
U8 = mybir.dt.uint8
FP8X4 = mybir.dt.float8_e4m3fn_x4

B, S, D, E = 2, 512, 512, 128
P = 128
PACK = 4
PAIRS = D // 2
HALVES = 2
ROWS = 2

BANK = 512

FLOPS = 2 * 2 * B * S * D * E
SCALE = 1.0 / math.sqrt(S)

K_GROUPS_ON_VECTOR = (84, 80)

WARM_PASSES = 3


def tile_efficientattention_s_kernel(tc, q, k, v, out):
    nc = tc.nc
    with ExitStack() as ctx:
        keep = ctx.enter_context(tc.tile_pool(name="keep", bufs=1))
        banks = ctx.enter_context(tc.psum_pool(name="banks", bufs=8))
        ctx.enter_context(tc.manual_schedule())

        def new_bank():
            bank = banks.tile([P, BANK], F32, name="bank")
            return bank

        v_raw = keep.tile([P, B, PACK, E], BF16)
        k_raw = {}
        q_raw = {}

        def load_v():
            nc.sync.dma_start(out=v_raw[:], in_=v.rearrange("b (p j) e -> p b j e", j=PACK))

        def load_k(b):
            k_raw[b] = keep.tile([P, PACK, D], BF16, name="k_raw%d" % b)
            nc.sync.dma_start(out=k_raw[b][:], in_=k[b].rearrange("(p j) d -> p j d", j=PACK))

        def load_q(b, h):
            rows = slice(h * ROWS * P, (h + 1) * ROWS * P)
            q_raw[(b, h)] = keep.tile([P, ROWS, D], BF16, name="q_raw%d%d" % (b, h))
            nc.sync.dma_start(
                out=q_raw[(b, h)][:],
                in_=q[b, rows, :].rearrange("(p r) d -> p r d", r=ROWS),
            )

        load_v()
        load_k(0)
        load_q(0, 0)
        load_k(1)
        load_q(0, 1)
        load_q(1, 0)
        load_q(1, 1)

        identity = keep.tile([P, P], F32)
        make_identity(nc, identity[:])

        v_grouped = keep.tile([P, B, E, PACK], BF16, align_bytes=64)
        v_codes = keep.tile([P, B * E], U32, align_bytes=64)
        v_scales = keep.tile([P, B * E], U8, align_bytes=64)
        k_grouped = {}
        k_codes = {}
        k_scales = {}
        kv_psum = {}
        kv_grouped = {}
        kv_codes = {}
        kv_scales = {}
        for b in range(B):
            k_grouped[b] = keep.tile([P, D, PACK], BF16, name="k_grouped%d" % b, align_bytes=64)
            k_codes[b] = keep.tile([P, D], U32, name="k_codes%d" % b, align_bytes=64)
            k_scales[b] = keep.tile([P, D], U8, name="k_scales%d" % b, align_bytes=64)
            kv_grouped[b] = keep.tile([P, E, PACK], BF16, name="kv_grouped%d" % b, align_bytes=64)
            kv_codes[b] = keep.tile([P, E], U32, name="kv_codes%d" % b, align_bytes=64)
            kv_scales[b] = keep.tile([P, E], U8, name="kv_scales%d" % b, align_bytes=64)
        q_grouped = {}
        q_codes = {}
        q_scales = {}
        out_sbuf = {}
        for bh in q_raw:
            q_grouped[bh] = keep.tile(
                [P, ROWS * P, PACK], BF16, name="q_grouped%d%d" % bh, align_bytes=64
            )
            q_codes[bh] = keep.tile([P, ROWS * P], U32, name="q_codes%d%d" % bh, align_bytes=64)
            q_scales[bh] = keep.tile([P, ROWS * P], U8, name="q_scales%d%d" % bh, align_bytes=64)
            out_sbuf[bh] = keep.tile([P, ROWS * E], F32, name="out_sbuf%d%d" % bh)

        def quantise(codes, scales, grouped, cols):
            nc.vector.quantize_mx(
                out=codes[:, cols].bitcast(FP8X4),
                scales=scales[:, cols],
                in_=grouped[:, cols.start * PACK : cols.stop * PACK],
            )

        def group_v(b):
            nc.vector.tensor_copy(
                out=v_grouped[:, b].rearrange("p (c i) j -> p c j i", i=8),
                in_=v_raw[:, b].rearrange("p j (c i) -> p c j i", i=8),
            )

        def quantise_v(b):
            quantise(
                v_codes,
                v_scales,
                v_grouped[:].rearrange("p b e j -> p (b e j)"),
                slice(b * E, (b + 1) * E),
            )

        def group_k(b, runs):
            source = k_raw[b][:].rearrange("p j (m t) -> p m j t", t=PACK)[:, :, :, runs]
            target = k_grouped[b][:].rearrange("p (t m) j -> p m j t", t=PACK)[:, :, :, runs]
            split = K_GROUPS_ON_VECTOR[b]
            nc.scalar.mul(out=target[:, split:], in_=source[:, split:], mul=SCALE)
            nc.vector.tensor_scalar_mul(
                out=target[:, :split], in0=source[:, :split], scalar1=SCALE
            )

        def quantise_k(b, half):
            quantise(
                k_codes[b],
                k_scales[b],
                k_grouped[b][:].rearrange("p c j -> p (c j)"),
                slice(half * D // 2, (half + 1) * D // 2),
            )

        def multiply_kv(b):
            kv_psum[b] = new_bank()
            value_cols = slice(b * E, (b + 1) * E)
            for t in range(PACK):
                feature_cols = slice(t * P, (t + 1) * P)
                nc.tensor.matmul_mx(
                    out=kv_psum[b][:, t * E : (t + 1) * E],
                    lhsT=k_codes[b][:, feature_cols].bitcast(FP8X4),
                    lhsT_scale=k_scales[b][:, feature_cols],
                    rhs=v_codes[:, value_cols].bitcast(FP8X4),
                    rhs_scale=v_scales[:, value_cols],
                    start=True,
                    stop=True,
                )

        def copy_kv(b, copy):
            copy(
                out=kv_grouped[b][:].rearrange("p (c i) t -> p c t i", i=2),
                in_=kv_psum[b][:].rearrange("p (t c i) -> p c t i", t=PACK, i=2),
            )

        def quantise_kv(b):
            quantise(
                kv_codes[b],
                kv_scales[b],
                kv_grouped[b][:].rearrange("p n t -> p (n t)"),
                slice(0, E),
            )

        qt_psum = {}
        out_psum = {}

        def transpose_q(piece):
            b, h, first, count = piece
            words = q_raw[(b, h)][:].rearrange("p r d -> p (r d)").bitcast(F32)
            bank = new_bank()
            qt_psum[piece] = bank
            for i in range(count):
                for u in range(2):
                    block = u * count + i
                    nc.tensor.transpose(
                        bank[:, block * P : (block + 1) * P],
                        words[:, (first + i) * PAIRS + u : (first + i + 1) * PAIRS : 2],
                        identity[:],
                    )

        def scale_q(piece, multiply):
            b, h, first, count = piece
            source = qt_psum[piece][:, : count * PAIRS].bitcast(BF16)
            target = q_grouped[(b, h)][:, first * P : (first + count) * P, :]
            multiply(
                target.rearrange("p m (u e) -> p m u e", e=2),
                source.rearrange("p (u m e) -> p m u e", u=2, e=2),
                SCALE,
            )

        def quantise_q(piece):
            b, h, first, count = piece
            quantise(
                q_codes[(b, h)],
                q_scales[(b, h)],
                q_grouped[(b, h)][:].rearrange("p m t -> p (m t)"),
                slice(first * P, (first + count) * P),
            )

        def multiply_out(piece):
            b, h, first, count = piece
            bank = new_bank()
            out_psum[piece] = bank
            for i in range(count):
                row_cols = slice((first + i) * P, (first + i + 1) * P)
                nc.tensor.matmul_mx(
                    out=bank[:, i * E : (i + 1) * E],
                    lhsT=q_codes[(b, h)][:, row_cols].bitcast(FP8X4),
                    lhsT_scale=q_scales[(b, h)][:, row_cols],
                    rhs=kv_codes[b][:].bitcast(FP8X4),
                    rhs_scale=kv_scales[b][:],
                    start=True,
                    stop=True,
                )

        def copy_out(piece, copy):
            b, h, first, count = piece
            copy(
                out=out_sbuf[(b, h)][:, first * E : (first + count) * E],
                in_=out_psum[piece][:, : count * E],
            )

        def store(piece):
            b, h, first, count = piece
            rows = out[b, h * ROWS * P : (h + 1) * ROWS * P, :]
            nc.sync.dma_start(
                out=rows.rearrange("(p r) e -> p r e", r=ROWS)[:, first : first + count, :],
                in_=out_sbuf[(b, h)][:, first * E : (first + count) * E].rearrange(
                    "p (r e) -> p r e", r=count
                ),
            )

        on_scalar = nc.scalar.mul
        on_vector = nc.vector.tensor_scalar_mul

        def warm_tensor():
            bank = new_bank()
            for i in range(WARM_PASSES):
                nc.tensor.matmul(
                    bank[:, i * P : (i + 1) * P],
                    identity[:],
                    identity[:],
                    start=True,
                    stop=True,
                )

        q00 = (0, 0, 0, 2)
        q00a = (0, 0, 0, 1)
        q00b = (0, 0, 1, 1)
        q01 = (0, 1, 0, 2)
        q10 = (1, 0, 0, 2)
        q11a = (1, 1, 0, 1)
        q11b = (1, 1, 1, 1)

        warm_tensor()
        group_v(0)
        group_v(1)
        quantise_v(0)
        quantise_v(1)
        group_k(0, slice(0, 2))
        group_k(0, slice(2, 4))
        quantise_k(0, 0)
        quantise_k(0, 1)
        transpose_q(q00a)
        transpose_q(q00b)
        multiply_kv(0)
        scale_q(q00a, on_scalar)
        scale_q(q00b, on_vector)
        group_k(1, slice(0, 4))
        transpose_q(q01)
        transpose_q(q10)
        quantise_q(q00)
        quantise_k(1, 0)
        quantise_k(1, 1)
        copy_kv(0, nc.scalar.copy)
        multiply_kv(1)
        transpose_q(q11a)
        transpose_q(q11b)
        scale_q(q01, on_scalar)
        quantise_kv(0)
        scale_q(q10, on_vector)
        multiply_out(q00)
        quantise_q(q01)
        multiply_out(q01)
        copy_kv(1, nc.scalar.copy)
        scale_q(q11a, on_scalar)
        quantise_q(q10)
        quantise_kv(1)
        scale_q(q11b, on_vector)
        multiply_out(q10)
        quantise_q(q11a)
        multiply_out(q11a)
        quantise_q(q11b)
        multiply_out(q11b)
        copy_out(q00, nc.scalar.copy)
        store(q00)
        copy_out(q01, nc.scalar.copy)
        store(q01)
        copy_out(q10, nc.scalar.copy)
        store(q10)
        copy_out(q11a, nc.vector.tensor_copy)
        store(q11a)
        copy_out(q11b, nc.vector.tensor_copy)
        store(q11b)
